import numpy as np
import ml_dtypes


def mxq(x, axis, fmt="e4m3"):
    dtype, down = {"e4m3": (ml_dtypes.float8_e4m3fn, 7), "e5m2": (ml_dtypes.float8_e5m2, 14)}[fmt]
    v = np.moveaxis(np.asarray(x, np.float32).astype(ml_dtypes.bfloat16).astype(np.float64), axis, -1)
    blocks = v.reshape(v.shape[:-1] + (-1, 32))
    amax = np.abs(blocks).max(-1, keepdims=True)
    byte = np.maximum(np.where(amax > 0, np.frexp(amax)[1] - 1 + 127, 0) - down, 1)
    scale = np.exp2(byte - 127.0)
    codes = (blocks / scale).astype(np.float32).astype(dtype).astype(np.float64)
    return np.moveaxis((codes * scale).reshape(v.shape), -1, axis)


WIDE = False


def mx_kscale(k, group=512):
    if not WIDE:
        return np.ones(k)
    levels = np.array([10, -10, 5, -5, 0])
    if group != 512:
        return np.exp2(np.random.permutation(np.resize(levels, k // group))).repeat(group)
    a = np.random.permutation(np.resize(levels, k // 512 * 4)).reshape(k // 512, 4)
    idx = np.arange(k)
    return np.exp2(a[idx // 512, idx % 128 // 32])


BF16 = ml_dtypes.bfloat16


def bf(x):
    return np.asarray(x, np.float32).astype(BF16)


def f64(x):
    return np.asarray(x).astype(np.float64)


B, C, H, W, KERNEL, M, O = 128, 3, 34, 34, 3, 1024, 128
K = C * KERNEL * KERNEL
HO, WO = H - KERNEL + 1, W - KERNEL + 1
L = HO * WO


def unfold(x):
    cols = [x[:, :, i:i + HO, j:j + WO] for i in range(KERNEL) for j in range(KERNEL)]
    return np.stack(cols, axis=2).reshape(B, K, L)


def setup_inputs():
    t = mx_kscale(M, group=M // 2)
    return {"x": bf(np.random.standard_normal((B, C, H, W))),
            "G": bf(np.random.standard_normal((M, L)) / np.sqrt(L) * t[:, None]),
            "v": bf(np.random.standard_normal((M, K, O)) * 0.7 / np.sqrt(K * M) / t[:, None, None]),
            "w": bf(np.random.standard_normal((M, K, O)) * 0.7 / np.sqrt(K * M) / t[:, None, None])}


def reference(x, G, v, w):
    U = unfold(f64(x))
    A = mxq(U, 2, "e4m3") @ mxq(f64(G), 1, "e4m3").T
    p_diff = f64(v) - f64(w)
    return mxq(A.reshape(B, K * M), 1, "e4m3") @ mxq(p_diff.transpose(1, 0, 2).reshape(K * M, O), 0, "e4m3")

@@ -1,0 +1,200 @@
+from contextlib import ExitStack
+
+import concourse.mybir as mybir
+from concourse.masks import make_identity
+
+F32 = mybir.dt.float32
+BF16 = mybir.dt.bfloat16
+U32 = mybir.dt.uint32
+U8 = mybir.dt.uint8
+FP8X4 = mybir.dt.float8_e4m3fn_x4
+
+P = 128
+FLOPS = 2 * (128 * 27 * 1024 * 1024 + 128 * 27 * 1024 * 128)
+
+ACT_COLS = 192
+VW_BUFS = 4
+
+
+def tile_convexrelucnn_kernel(tc, x, G, v, w, out):
+    nc = tc.nc
+    with ExitStack() as ctx:
+        const = ctx.enter_context(tc.tile_pool(name="const", bufs=1))
+        stage = ctx.enter_context(tc.tile_pool(name="stage", bufs=3))
+        vw = ctx.enter_context(tc.tile_pool(name="vw", bufs=VW_BUFS))
+        psum = ctx.enter_context(tc.psum_pool(name="psum", bufs=7))
+        psum_acc = ctx.enter_context(tc.psum_pool(name="psum_acc", bufs=1))
+
+        chunks = [(g, c) for g in range(2) for c in range(3)]
+
+        x_rows = x.rearrange("b c r s -> b c (r s)")
+        x_raw = []
+        for c in range(3):
+            xr = const.tile([P, 1156], BF16, name="x_raw%d" % c)
+            nc.sync.dma_start(out=xr[:], in_=x_rows[:, c, :])
+            x_raw.append(xr)
+        g_rows = G.rearrange("(g p t) n -> p g (t n)", g=2, t=4)
+        g_raw = []
+        for g in range(2):
+            gr = const.tile([P, 4096], BF16, name="g_raw%d" % g)
+            nc.sync.dma_start(out=gr[:], in_=g_rows[:, g, :])
+            g_raw.append(gr)
+        v_rows = v.rearrange("(g p t) k o -> p g t (k o)", g=2, t=4)
+        w_rows = w.rearrange("(g p t) k o -> p g t (k o)", g=2, t=4)
+        vw_tiles = {}
+
+        def load_chunk(n):
+            g, c = chunks[n]
+            v_t = vw.tile([P, 4608], BF16, name="v_t", tag="v_t", align_bytes=64)
+            w_t = vw.tile([P, 4608], BF16, name="w_t", tag="w_t", align_bytes=64)
+            nc.sync.dma_start(
+                out=v_t[:].rearrange("p (t q) -> p t q", t=4),
+                in_=v_rows[:, g, :, 1152 * c : 1152 * (c + 1)],
+            )
+            nc.sync.dma_start(
+                out=w_t[:].rearrange("p (t q) -> p t q", t=4),
+                in_=w_rows[:, g, :, 1152 * c : 1152 * (c + 1)],
+            )
+            vw_tiles[n] = (v_t, w_t)
+
+        for n in range(VW_BUFS):
+            load_chunk(n)
+
+        ident = const.tile([P, P], F32, name="ident")
+        make_identity(nc, ident[:])
+
+        g_codes = const.tile([P, 16 * P], U32, name="g_codes", align_bytes=64)
+        g_scales = const.tile([P, 16 * P], U8, name="g_scales", align_bytes=64)
+        u_codes = const.tile([P, 36 * P], U32, name="u_codes", align_bytes=64)
+        u_scales = const.tile([P, 36 * P], U8, name="u_scales", align_bytes=64)
+
+        def copy_out(dst, src):
+            nc.scalar.copy(out=dst, in_=src)
+
+        def transpose_and_quantise(words, offsets, codes, scales):
+            grp = stage.tile([P, 2048], BF16, name="grp", tag="grp", align_bytes=64)
+            grp_w = grp[:].bitcast(F32).rearrange("p (s b u) -> p s b u", s=4, u=2)
+            for h in range(2):
+                bank = psum.tile([P, 512], F32, name="bank", tag="bank")
+                for s in range(2):
+                    for u in range(2):
+                        off = offsets[2 * h + s] + P * u
+                        col = (2 * s + u) * P
+                        nc.tensor.transpose(bank[:, col : col + P], words[:, off : off + P], ident[:])
+                copy_out(
+                    grp_w[:, 2 * h : 2 * h + 2],
+                    bank[:].rearrange("p (s u b) -> p s b u", s=2, u=2),
+                )
+            nc.vector.quantize_mx(out=codes.bitcast(FP8X4), scales=scales, in_=grp[:])
+
+        def prep_u(c):
+            xj = const.tile([P, 3264], BF16, name="xj%d" % c, align_bytes=64)
+            src = x_raw[c][:].rearrange("p (r2 par s) -> p par r2 s", par=2, s=34)
+            dst = xj[:].rearrange("p (j par r2 wo) -> p j par r2 wo", j=3, par=2, wo=32)
+            nc.vector.tensor_copy(out=dst[:, 0], in_=src[:, :, :, 0:32])
+            nc.scalar.copy(out=dst[:, 1], in_=src[:, :, :, 1:33])
+            nc.vector.tensor_copy(out=dst[:, 2], in_=src[:, :, :, 2:34])
+            words = xj[:].bitcast(F32)
+            for j in range(3):
+                offsets = [((j * 2 + rho % 2) * 17 + rho // 2) * 16 for rho in range(4)]
+                lo = (c * 3 + j) * 4 * P
+                transpose_and_quantise(words, offsets, u_codes[:, lo : lo + 512], u_scales[:, lo : lo + 512])
+
+        def prep_g(g):
+            gd = const.tile([P, 4096], BF16, name="g_split%d" % g, align_bytes=64)
+            src = g_raw[g][:].rearrange("p (t a par wo) -> p t par a wo", t=4, par=2, wo=32)
+            dst = gd[:].rearrange("p (t par a wo) -> p t par a wo", t=4, par=2, wo=32)
+            for par in range(2):
+                nc.vector.tensor_copy(out=dst[:, :, par], in_=src[:, :, par])
+            words = gd[:].bitcast(F32)
+            for par in range(2):
+                offsets = [(t * 2 + par) * 256 for t in range(4)]
+                lo = (par * 2 + g) * 4 * P
+                transpose_and_quantise(words, offsets, g_codes[:, lo : lo + 512], g_scales[:, lo : lo + 512])
+
+        acc = psum_acc.tile([P, P], F32, name="acc")
+
+        def p_chain(n):
+            v_t, w_t = vw_tiles[n]
+            nc.vector.tensor_tensor(out=v_t[:], in0=v_t[:], in1=w_t[:], op=mybir.AluOpType.subtract)
+            split = 1152 - ACT_COLS
+            d_rows = v_t[:].rearrange("p (t q) -> p t q", t=4)
+            nc.vector.tensor_copy(
+                out=w_t[:, 0 : 4 * split].rearrange("p (q i t) -> p q t i", i=4, t=4),
+                in_=d_rows[:, :, 0:split].rearrange("p t (q i) -> p q t i", i=4),
+            )
+            nc.scalar.copy(
+                out=w_t[:, 4 * split : 4608].rearrange("p (q i t) -> p q t i", i=4, t=4),
+                in_=d_rows[:, :, split:1152].rearrange("p t (q i) -> p q t i", i=4),
+            )
+            p_codes = stage.tile([P, 1152], U32, name="p_codes", tag="p_codes", align_bytes=64)
+            p_scales = stage.tile([P, 1152], U8, name="p_scales", tag="p_scales", align_bytes=64)
+            nc.vector.quantize_mx(
+                out=p_codes[:, 0:1024].bitcast(FP8X4), scales=p_scales[:, 0:1024], in_=w_t[:, 0:4096]
+            )
+            nc.vector.quantize_mx(
+                out=p_codes[:, 1024:1152].bitcast(FP8X4), scales=p_scales[:, 1024:1152], in_=w_t[:, 4096:4608]
+            )
+            return p_codes, p_scales
+
+        def first_matmul(n):
+            g, c = chunks[n]
+            a_codes = stage.tile([P, 1152], U32, name="a_codes", tag="a_codes", align_bytes=64)
+            a_scales = stage.tile([P, 1152], U8, name="a_scales", tag="a_scales", align_bytes=64)
+            for first, count in ((0, 4), (4, 4), (8, 1)):
+                ag = stage.tile([P, 2048], BF16, name="ag", tag="ag", align_bytes=64)
+                for s in range(count):
+                    i, j = divmod(first + s, 3)
+                    bank = psum.tile([P, 512], F32, name="bank", tag="bank")
+                    for t in range(4):
+                        for par in range(2):
+                            gi = ((par * 2 + g) * 4 + t) * P
+                            ui = ((c * 3 + j) * 4 + i + par) * P
+                            nc.tensor.matmul_mx(
+                                out=bank[:, t * P : (t + 1) * P],
+                                lhsT=g_codes[:, gi : gi + P].bitcast(FP8X4),
+                                lhsT_scale=g_scales[:, gi : gi + P],
+                                rhs=u_codes[:, ui : ui + P].bitcast(FP8X4),
+                                rhs_scale=u_scales[:, ui : ui + P],
+                                start=(par == 0),
+                                stop=(par == 1),
+                            )
+                    copy_out(
+                        ag[:, s * 512 : (s + 1) * 512].rearrange("p (b t) -> p b t", t=4),
+                        bank[:].rearrange("p (t b) -> p b t", t=4),
+                    )
+                nc.vector.quantize_mx(
+                    out=a_codes[:, first * P : (first + count) * P].bitcast(FP8X4),
+                    scales=a_scales[:, first * P : (first + count) * P],
+                    in_=ag[:, 0 : count * 512],
+                )
+            return a_codes, a_scales
+
+        def second_matmul(n, a_codes, a_scales, p_codes, p_scales):
+            for kk in range(9):
+                cols = slice(kk * P, (kk + 1) * P)
+                nc.tensor.matmul_mx(
+                    out=acc[:],
+                    lhsT=a_codes[:, cols].bitcast(FP8X4),
+                    lhsT_scale=a_scales[:, cols],
+                    rhs=p_codes[:, cols].bitcast(FP8X4),
+                    rhs_scale=p_scales[:, cols],
+                    start=(n == 0 and kk == 0),
+                    stop=(n == len(chunks) - 1 and kk == 8),
+                )
+
+        prep_u(0)
+        prep_g(0)
+        later = {0: lambda: prep_u(1), 1: lambda: prep_u(2), 2: lambda: prep_g(1)}
+        for n in range(len(chunks)):
+            if n in later:
+                later[n]()
+            p_codes, p_scales = p_chain(n)
+            if n + VW_BUFS < len(chunks):
+                load_chunk(n + VW_BUFS)
+            a_codes, a_scales = first_matmul(n)
+            second_matmul(n, a_codes, a_scales, p_codes, p_scales)
+
+        res = const.tile([P, P], F32, name="res")
+        nc.vector.tensor_copy(out=res[:], in_=acc[:])
+        nc.sync.dma_start(out=out[:, :], in_=res[:])

@@ -12,8 +12,9 @@ FP8X4 = mybir.dt.float8_e4m3fn_x4
 P = 128
 FLOPS = 2 * (128 * 27 * 1024 * 1024 + 128 * 27 * 1024 * 128)
 
-ACT_COLS = 192
+ACT_COLS = (192, 384)
 VW_BUFS = 4
+J_ORDER = (0, 2, 1)
 
 
 def tile_convexrelucnn_kernel(tc, x, G, v, w, out):
@@ -24,24 +25,33 @@ def tile_convexrelucnn_kernel(tc, x, G, v, w, out):
         vw = ctx.enter_context(tc.tile_pool(name="vw", bufs=VW_BUFS))
         psum = ctx.enter_context(tc.psum_pool(name="psum", bufs=7))
         psum_acc = ctx.enter_context(tc.psum_pool(name="psum_acc", bufs=1))
+        ctx.enter_context(tc.manual_schedule())
 
         chunks = [(g, c) for g in range(2) for c in range(3)]
 
         x_rows = x.rearrange("b c r s -> b c (r s)")
-        x_raw = []
-        for c in range(3):
-            xr = const.tile([P, 1156], BF16, name="x_raw%d" % c)
-            nc.sync.dma_start(out=xr[:], in_=x_rows[:, c, :])
-            x_raw.append(xr)
         g_rows = G.rearrange("(g p t) n -> p g (t n)", g=2, t=4)
-        g_raw = []
-        for g in range(2):
-            gr = const.tile([P, 4096], BF16, name="g_raw%d" % g)
-            nc.sync.dma_start(out=gr[:], in_=g_rows[:, g, :])
-            g_raw.append(gr)
         v_rows = v.rearrange("(g p t) k o -> p g t (k o)", g=2, t=4)
         w_rows = w.rearrange("(g p t) k o -> p g t (k o)", g=2, t=4)
+        x_raw = {}
+        g_raw = {}
+        xj = {}
+        gd = {}
         vw_tiles = {}
+        grp_of = {}
+        a_of = {}
+        p_of = {}
+        ag_of = {}
+
+        def load_x(c):
+            xr = const.tile([P, 1156], BF16, name="x_raw%d" % c)
+            nc.sync.dma_start(out=xr[:], in_=x_rows[:, c, :])
+            x_raw[c] = xr
+
+        def load_g(g):
+            gr = const.tile([P, 4096], BF16, name="g_raw%d" % g)
+            nc.sync.dma_start(out=gr[:], in_=g_rows[:, g, :])
+            g_raw[g] = gr
 
         def load_chunk(n):
             g, c = chunks[n]
@@ -57,7 +67,13 @@ def tile_convexrelucnn_kernel(tc, x, G, v, w, out):
             )
             vw_tiles[n] = (v_t, w_t)
 
-        for n in range(VW_BUFS):
+        load_x(0)
+        load_g(0)
+        load_x(1)
+        load_x(2)
+        load_chunk(0)
+        load_g(1)
+        for n in range(1, VW_BUFS):
             load_chunk(n)
 
         ident = const.tile([P, P], F32, name="ident")
@@ -67,12 +83,36 @@ def tile_convexrelucnn_kernel(tc, x, G, v, w, out):
         g_scales = const.tile([P, 16 * P], U8, name="g_scales", align_bytes=64)
         u_codes = const.tile([P, 36 * P], U32, name="u_codes", align_bytes=64)
         u_scales = const.tile([P, 36 * P], U8, name="u_scales", align_bytes=64)
+        acc = psum_acc.tile([P, P], F32, name="acc")
 
-        def copy_out(dst, src):
-            nc.scalar.copy(out=dst, in_=src)
+        def compact(c, j, on_scalar):
+            if c not in xj:
+                xj_c = const.tile([P, 3264], BF16, name="xj%d" % c, align_bytes=64)
+                xj[c] = xj_c
+            src = x_raw[c][:].rearrange("p (r2 par s) -> p par r2 s", par=2, s=34)
+            dst = xj[c][:].rearrange("p (j par r2 wo) -> p j par r2 wo", j=3, par=2, wo=32)
+            if on_scalar:
+                nc.scalar.copy(out=dst[:, j], in_=src[:, :, :, j : j + 32])
+            else:
+                nc.vector.tensor_copy(out=dst[:, j], in_=src[:, :, :, j : j + 32])
 
-        def transpose_and_quantise(words, offsets, codes, scales):
+        def split_g(g):
+            gd_g = const.tile([P, 4096], BF16, name="g_split%d" % g, align_bytes=64)
+            gd[g] = gd_g
+            src = g_raw[g][:].rearrange("p (t a par wo) -> p t par a wo", t=4, par=2, wo=32)
+            dst = gd_g[:].rearrange("p (t par a wo) -> p t par a wo", t=4, par=2, wo=32)
+            for par in range(2):
+                nc.vector.tensor_copy(out=dst[:, :, par], in_=src[:, :, par])
+
+        def transpose_unit(kind, a, b):
+            if kind == "U":
+                words = xj[a][:].bitcast(F32)
+                offsets = [((b * 2 + rho % 2) * 17 + rho // 2) * 16 for rho in range(4)]
+            else:
+                words = gd[a][:].bitcast(F32)
+                offsets = [(t * 2 + b) * 256 for t in range(4)]
             grp = stage.tile([P, 2048], BF16, name="grp", tag="grp", align_bytes=64)
+            grp_of[(kind, a, b)] = grp
             grp_w = grp[:].bitcast(F32).rearrange("p (s b u) -> p s b u", s=4, u=2)
             for h in range(2):
                 bank = psum.tile([P, 512], F32, name="bank", tag="bank")
@@ -81,96 +121,94 @@ def tile_convexrelucnn_kernel(tc, x, G, v, w, out):
                         off = offsets[2 * h + s] + P * u
                         col = (2 * s + u) * P
                         nc.tensor.transpose(bank[:, col : col + P], words[:, off : off + P], ident[:])
-                copy_out(
-                    grp_w[:, 2 * h : 2 * h + 2],
-                    bank[:].rearrange("p (s u b) -> p s b u", s=2, u=2),
+                nc.scalar.copy(
+                    out=grp_w[:, 2 * h : 2 * h + 2],
+                    in_=bank[:].rearrange("p (s u b) -> p s b u", s=2, u=2),
                 )
-            nc.vector.quantize_mx(out=codes.bitcast(FP8X4), scales=scales, in_=grp[:])
 
-        def prep_u(c):
-            xj = const.tile([P, 3264], BF16, name="xj%d" % c, align_bytes=64)
-            src = x_raw[c][:].rearrange("p (r2 par s) -> p par r2 s", par=2, s=34)
-            dst = xj[:].rearrange("p (j par r2 wo) -> p j par r2 wo", j=3, par=2, wo=32)
-            nc.vector.tensor_copy(out=dst[:, 0], in_=src[:, :, :, 0:32])
-            nc.scalar.copy(out=dst[:, 1], in_=src[:, :, :, 1:33])
-            nc.vector.tensor_copy(out=dst[:, 2], in_=src[:, :, :, 2:34])
-            words = xj[:].bitcast(F32)
-            for j in range(3):
-                offsets = [((j * 2 + rho % 2) * 17 + rho // 2) * 16 for rho in range(4)]
-                lo = (c * 3 + j) * 4 * P
-                transpose_and_quantise(words, offsets, u_codes[:, lo : lo + 512], u_scales[:, lo : lo + 512])
+        def quantise_unit(kind, a, b):
+            grp = grp_of[(kind, a, b)]
+            if kind == "U":
+                lo = (a * 3 + b) * 512
+                codes, scales = u_codes, u_scales
+            else:
+                lo = (b * 2 + a) * 512
+                codes, scales = g_codes, g_scales
+            nc.vector.quantize_mx(
+                out=codes[:, lo : lo + 512].bitcast(FP8X4), scales=scales[:, lo : lo + 512], in_=grp[:]
+            )
 
-        def prep_g(g):
-            gd = const.tile([P, 4096], BF16, name="g_split%d" % g, align_bytes=64)
-            src = g_raw[g][:].rearrange("p (t a par wo) -> p t par a wo", t=4, par=2, wo=32)
-            dst = gd[:].rearrange("p (t par a wo) -> p t par a wo", t=4, par=2, wo=32)
-            for par in range(2):
-                nc.vector.tensor_copy(out=dst[:, :, par], in_=src[:, :, par])
-            words = gd[:].bitcast(F32)
-            for par in range(2):
-                offsets = [(t * 2 + par) * 256 for t in range(4)]
-                lo = (par * 2 + g) * 4 * P
-                transpose_and_quantise(words, offsets, g_codes[:, lo : lo + 512], g_scales[:, lo : lo + 512])
-
-        acc = psum_acc.tile([P, P], F32, name="acc")
-
-        def p_chain(n):
+        def subtract(n):
             v_t, w_t = vw_tiles[n]
             nc.vector.tensor_tensor(out=v_t[:], in0=v_t[:], in1=w_t[:], op=mybir.AluOpType.subtract)
-            split = 1152 - ACT_COLS
-            d_rows = v_t[:].rearrange("p (t q) -> p t q", t=4)
-            nc.vector.tensor_copy(
-                out=w_t[:, 0 : 4 * split].rearrange("p (q i t) -> p q t i", i=4, t=4),
-                in_=d_rows[:, :, 0:split].rearrange("p t (q i) -> p q t i", i=4),
-            )
-            nc.scalar.copy(
-                out=w_t[:, 4 * split : 4608].rearrange("p (q i t) -> p q t i", i=4, t=4),
-                in_=d_rows[:, :, split:1152].rearrange("p t (q i) -> p q t i", i=4),
-            )
+
+        def regroup(n, on_scalar):
+            v_t, w_t = vw_tiles[n]
+            split = 1152 - ACT_COLS[chunks[n][0]]
+            lo, hi = (split, 1152) if on_scalar else (0, split)
+            dst = w_t[:, 4 * lo : 4 * hi].rearrange("p (q i t) -> p q t i", i=4, t=4)
+            src = v_t[:].rearrange("p (t q) -> p t q", t=4)[:, :, lo:hi].rearrange("p t (q i) -> p q t i", i=4)
+            if on_scalar:
+                nc.scalar.copy(out=dst, in_=src)
+            else:
+                nc.vector.tensor_copy(out=dst, in_=src)
+
+        def quantise_p(n):
+            w_t = vw_tiles[n][1]
             p_codes = stage.tile([P, 1152], U32, name="p_codes", tag="p_codes", align_bytes=64)
             p_scales = stage.tile([P, 1152], U8, name="p_scales", tag="p_scales", align_bytes=64)
+            p_of[n] = (p_codes, p_scales)
             nc.vector.quantize_mx(
                 out=p_codes[:, 0:1024].bitcast(FP8X4), scales=p_scales[:, 0:1024], in_=w_t[:, 0:4096]
             )
             nc.vector.quantize_mx(
                 out=p_codes[:, 1024:1152].bitcast(FP8X4), scales=p_scales[:, 1024:1152], in_=w_t[:, 4096:4608]
             )
-            return p_codes, p_scales
 
-        def first_matmul(n):
+        def first_matmul(n, kk):
             g, c = chunks[n]
-            a_codes = stage.tile([P, 1152], U32, name="a_codes", tag="a_codes", align_bytes=64)
-            a_scales = stage.tile([P, 1152], U8, name="a_scales", tag="a_scales", align_bytes=64)
-            for first, count in ((0, 4), (4, 4), (8, 1)):
+            if kk % 4 == 0:
                 ag = stage.tile([P, 2048], BF16, name="ag", tag="ag", align_bytes=64)
-                for s in range(count):
-                    i, j = divmod(first + s, 3)
-                    bank = psum.tile([P, 512], F32, name="bank", tag="bank")
-                    for t in range(4):
-                        for par in range(2):
-                            gi = ((par * 2 + g) * 4 + t) * P
-                            ui = ((c * 3 + j) * 4 + i + par) * P
-                            nc.tensor.matmul_mx(
-                                out=bank[:, t * P : (t + 1) * P],
-                                lhsT=g_codes[:, gi : gi + P].bitcast(FP8X4),
-                                lhsT_scale=g_scales[:, gi : gi + P],
-                                rhs=u_codes[:, ui : ui + P].bitcast(FP8X4),
-                                rhs_scale=u_scales[:, ui : ui + P],
-                                start=(par == 0),
-                                stop=(par == 1),
-                            )
-                    copy_out(
-                        ag[:, s * 512 : (s + 1) * 512].rearrange("p (b t) -> p b t", t=4),
-                        bank[:].rearrange("p (t b) -> p b t", t=4),
+                ag_of[(n, kk // 4)] = ag
+            ag = ag_of[(n, kk // 4)]
+            s = kk % 4
+            i, j = divmod(kk, 3)
+            bank = psum.tile([P, 512], F32, name="bank", tag="bank")
+            for t in range(4):
+                for par in range(2):
+                    gi = ((par * 2 + g) * 4 + t) * P
+                    ui = ((c * 3 + j) * 4 + i + par) * P
+                    nc.tensor.matmul_mx(
+                        out=bank[:, t * P : (t + 1) * P],
+                        lhsT=g_codes[:, gi : gi + P].bitcast(FP8X4),
+                        lhsT_scale=g_scales[:, gi : gi + P],
+                        rhs=u_codes[:, ui : ui + P].bitcast(FP8X4),
+                        rhs_scale=u_scales[:, ui : ui + P],
+                        start=(par == 0),
+                        stop=(par == 1),
                     )
-                nc.vector.quantize_mx(
-                    out=a_codes[:, first * P : (first + count) * P].bitcast(FP8X4),
-                    scales=a_scales[:, first * P : (first + count) * P],
-                    in_=ag[:, 0 : count * 512],
-                )
-            return a_codes, a_scales
+            nc.scalar.copy(
+                out=ag[:, s * 512 : (s + 1) * 512].rearrange("p (b t) -> p b t", t=4),
+                in_=bank[:].rearrange("p (t b) -> p b t", t=4),
+            )
 
-        def second_matmul(n, a_codes, a_scales, p_codes, p_scales):
+        def quantise_a(n, grp_i):
+            if grp_i == 0:
+                a_codes = stage.tile([P, 1152], U32, name="a_codes", tag="a_codes", align_bytes=64)
+                a_scales = stage.tile([P, 1152], U8, name="a_scales", tag="a_scales", align_bytes=64)
+                a_of[n] = (a_codes, a_scales)
+            a_codes, a_scales = a_of[n]
+            count = 4 if grp_i < 2 else 1
+            lo = grp_i * 512
+            nc.vector.quantize_mx(
+                out=a_codes[:, lo : lo + count * P].bitcast(FP8X4),
+                scales=a_scales[:, lo : lo + count * P],
+                in_=ag_of[(n, grp_i)][:, 0 : count * 512],
+            )
+
+        def second_matmul(n):
+            a_codes, a_scales = a_of[n]
+            p_codes, p_scales = p_of[n]
             for kk in range(9):
                 cols = slice(kk * P, (kk + 1) * P)
                 nc.tensor.matmul_mx(
@@ -183,17 +221,61 @@ def tile_convexrelucnn_kernel(tc, x, G, v, w, out):
                     stop=(n == len(chunks) - 1 and kk == 8),
                 )
 
-        prep_u(0)
-        prep_g(0)
-        later = {0: lambda: prep_u(1), 1: lambda: prep_u(2), 2: lambda: prep_g(1)}
+        compact(0, 0, False)
+        compact(0, 2, False)
+        compact(0, 1, True)
+        for j in J_ORDER:
+            transpose_unit("U", 0, j)
+        split_g(0)
+        for c in (1, 2):
+            compact(c, 0, False)
+            compact(c, 2, False)
+        for j in J_ORDER:
+            quantise_unit("U", 0, j)
+        compact(1, 1, True)
+        for par in range(2):
+            transpose_unit("G", 0, par)
+        compact(2, 1, True)
+        for par in range(2):
+            quantise_unit("G", 0, par)
+        for j in J_ORDER:
+            transpose_unit("U", 1, j)
+        subtract(0)
+        for j in J_ORDER:
+            quantise_unit("U", 1, j)
+
         for n in range(len(chunks)):
-            if n in later:
-                later[n]()
-            p_codes, p_scales = p_chain(n)
+            for kk in range(4):
+                first_matmul(n, kk)
+            if n > 0:
+                second_matmul(n - 1)
+            regroup(n, True)
+            for kk in range(4, 9):
+                first_matmul(n, kk)
+            if n == 0:
+                for j in J_ORDER:
+                    transpose_unit("U", 2, j)
+            if n == 1:
+                for par in range(2):
+                    transpose_unit("G", 1, par)
+            regroup(n, False)
+            quantise_a(n, 0)
+            quantise_p(n)
             if n + VW_BUFS < len(chunks):
                 load_chunk(n + VW_BUFS)
-            a_codes, a_scales = first_matmul(n)
-            second_matmul(n, a_codes, a_scales, p_codes, p_scales)
+            if n == 0:
+                split_g(1)
+            if n + 1 < len(chunks):
+                subtract(n + 1)
+            if n == 0:
+                for j in J_ORDER:
+                    quantise_unit("U", 2, j)
+            if n == 1:
+                for par in range(2):
+                    quantise_unit("G", 1, par)
+            quantise_a(n, 1)
+            quantise_a(n, 2)
+        second_matmul(len(chunks) - 1)
 
         res = const.tile([P, P], F32, name="res")
         nc.vector.tensor_copy(out=res[:], in_=acc[:])

@@ -12,8 +12,8 @@ FP8X4 = mybir.dt.float8_e4m3fn_x4
 P = 128
 FLOPS = 2 * (128 * 27 * 1024 * 1024 + 128 * 27 * 1024 * 128)
 
-ACT_COLS = (192, 384)
-VW_BUFS = 4
+ACT_COLS = (256, 384)
+VW_BUFS = 3
 J_ORDER = (0, 2, 1)
 
 
@@ -68,9 +68,9 @@ def tile_convexrelucnn_kernel(tc, x, G, v, w, out):
             vw_tiles[n] = (v_t, w_t)
 
         load_x(0)
-        load_g(0)
         load_x(1)
         load_x(2)
+        load_g(0)
         load_chunk(0)
         load_g(1)
         for n in range(1, VW_BUFS):
@@ -111,7 +111,7 @@ def tile_convexrelucnn_kernel(tc, x, G, v, w, out):
             else:
                 words = gd[a][:].bitcast(F32)
                 offsets = [(t * 2 + b) * 256 for t in range(4)]
-            grp = stage.tile([P, 2048], BF16, name="grp", tag="grp", align_bytes=64)
+            grp = stage.tile([P, 2048], BF16, name="grp", tag="grp", bufs=4, align_bytes=64)
             grp_of[(kind, a, b)] = grp
             grp_w = grp[:].bitcast(F32).rearrange("p (s b u) -> p s b u", s=4, u=2)
             for h in range(2):
@@ -168,7 +168,7 @@ def tile_convexrelucnn_kernel(tc, x, G, v, w, out):
         def first_matmul(n, kk):
             g, c = chunks[n]
             if kk % 4 == 0:
-                ag = stage.tile([P, 2048], BF16, name="ag", tag="ag", align_bytes=64)
+                ag = stage.tile([P, 2048], BF16, name="ag", tag="ag", bufs=4, align_bytes=64)
                 ag_of[(n, kk // 4)] = ag
             ag = ag_of[(n, kk // 4)]
             s = kk % 4
@@ -226,16 +226,14 @@ def tile_convexrelucnn_kernel(tc, x, G, v, w, out):
         compact(0, 1, True)
         for j in J_ORDER:
             transpose_unit("U", 0, j)
-        split_g(0)
         for c in (1, 2):
-            compact(c, 0, False)
-            compact(c, 2, False)
+            for j in J_ORDER:
+                compact(c, j, False)
+        split_g(0)
         for j in J_ORDER:
             quantise_unit("U", 0, j)
-        compact(1, 1, True)
         for par in range(2):
             transpose_unit("G", 0, par)
-        compact(2, 1, True)
         for par in range(2):
             quantise_unit("G", 0, par)
         for j in J_ORDER:
@@ -245,12 +243,13 @@ def tile_convexrelucnn_kernel(tc, x, G, v, w, out):
             quantise_unit("U", 1, j)
 
         for n in range(len(chunks)):
-            for kk in range(4):
+            for kk in range(5):
                 first_matmul(n, kk)
+            regroup(n, True)
+            first_matmul(n, 5)
             if n > 0:
                 second_matmul(n - 1)
-            regroup(n, True)
-            for kk in range(4, 9):
+            for kk in range(6, 9):
                 first_matmul(n, kk)
             if n == 0:
                 for j in J_ORDER:

@@ -12,7 +12,9 @@ FP8X4 = mybir.dt.float8_e4m3fn_x4
 P = 128
 FLOPS = 2 * (128 * 27 * 1024 * 1024 + 128 * 27 * 1024 * 128)
 
-ACT_COLS = (256, 384)
+PE_COLS = 256
+ALU_COLS = 1152 - PE_COLS
+ACT_COLS = (128, 192)
 VW_BUFS = 3
 J_ORDER = (0, 2, 1)
 
@@ -42,6 +44,7 @@ def tile_convexrelucnn_kernel(tc, x, G, v, w, out):
         a_of = {}
         p_of = {}
         ag_of = {}
+        pg_of = {}
 
         def load_x(c):
             xr = const.tile([P, 1156], BF16, name="x_raw%d" % c)
@@ -78,6 +81,12 @@ def tile_convexrelucnn_kernel(tc, x, G, v, w, out):
 
         ident = const.tile([P, P], F32, name="ident")
         make_identity(nc, ident[:])
+        plus = const.tile([P, P], BF16, name="plus")
+        minus = const.tile([P, P], BF16, name="minus")
+        nc.gpsimd.tensor_copy(out=plus[:], in_=ident[:])
+        nc.gpsimd.tensor_scalar(
+            out=minus[:], in0=ident[:], scalar1=-1.0, scalar2=0.0, op0=mybir.AluOpType.mult, op1=mybir.AluOpType.add
+        )
 
         g_codes = const.tile([P, 16 * P], U32, name="g_codes", align_bytes=64)
         g_scales = const.tile([P, 16 * P], U8, name="g_scales", align_bytes=64)
@@ -140,13 +149,33 @@ def tile_convexrelucnn_kernel(tc, x, G, v, w, out):
 
         def subtract(n):
             v_t, w_t = vw_tiles[n]
-            nc.vector.tensor_tensor(out=v_t[:], in0=v_t[:], in1=w_t[:], op=mybir.AluOpType.subtract)
+            v_cols = v_t[:].rearrange("p (t q) -> p t q", t=4)[:, :, 0:ALU_COLS]
+            w_cols = w_t[:].rearrange("p (t q) -> p t q", t=4)[:, :, 0:ALU_COLS]
+            nc.vector.tensor_tensor(out=v_cols, in0=v_cols, in1=w_cols, op=mybir.AluOpType.subtract)
+
+        def subtract_on_tensor(n):
+            v_t, w_t = vw_tiles[n]
+            v_q = v_t[:].rearrange("p (t q) -> p q t", t=4)
+            w_q = w_t[:].rearrange("p (t q) -> p q t", t=4)
+            pbank = psum.tile([P, 1024], BF16, name="pbank", tag="bank")
+            for h in range(PE_COLS // P):
+                cols = slice(ALU_COLS + h * P, ALU_COLS + (h + 1) * P)
+                dst = pbank[:, h * 512 : (h + 1) * 512].rearrange("p (q t) -> p q t", t=4)
+                nc.tensor.matmul(dst, lhsT=plus[:], rhs=v_q[:, cols], start=True, stop=False)
+                nc.tensor.matmul(dst, lhsT=minus[:], rhs=w_q[:, cols], start=False, stop=True)
+            nc.scalar.copy(out=p_grp(n)[:, 4 * ALU_COLS :], in_=pbank[:])
+
+        def p_grp(n):
+            if n not in pg_of:
+                pg = stage.tile([P, 4608], BF16, name="pg", tag="pg", bufs=2, align_bytes=64)
+                pg_of[n] = pg
+            return pg_of[n]
 
         def regroup(n, on_scalar):
-            v_t, w_t = vw_tiles[n]
-            split = 1152 - ACT_COLS[chunks[n][0]]
-            lo, hi = (split, 1152) if on_scalar else (0, split)
-            dst = w_t[:, 4 * lo : 4 * hi].rearrange("p (q i t) -> p q t i", i=4, t=4)
+            v_t = vw_tiles[n][0]
+            split = ALU_COLS - ACT_COLS[chunks[n][0]]
+            lo, hi = (split, ALU_COLS) if on_scalar else (0, split)
+            dst = p_grp(n)[:, 4 * lo : 4 * hi].rearrange("p (q i t) -> p q t i", i=4, t=4)
             src = v_t[:].rearrange("p (t q) -> p t q", t=4)[:, :, lo:hi].rearrange("p t (q i) -> p q t i", i=4)
             if on_scalar:
                 nc.scalar.copy(out=dst, in_=src)
@@ -154,15 +183,15 @@ def tile_convexrelucnn_kernel(tc, x, G, v, w, out):
                 nc.vector.tensor_copy(out=dst, in_=src)
 
         def quantise_p(n):
-            w_t = vw_tiles[n][1]
+            pg = p_grp(n)
             p_codes = stage.tile([P, 1152], U32, name="p_codes", tag="p_codes", align_bytes=64)
             p_scales = stage.tile([P, 1152], U8, name="p_scales", tag="p_scales", align_bytes=64)
             p_of[n] = (p_codes, p_scales)
             nc.vector.quantize_mx(
-                out=p_codes[:, 0:1024].bitcast(FP8X4), scales=p_scales[:, 0:1024], in_=w_t[:, 0:4096]
+                out=p_codes[:, 0:1024].bitcast(FP8X4), scales=p_scales[:, 0:1024], in_=pg[:, 0:4096]
             )
             nc.vector.quantize_mx(
-                out=p_codes[:, 1024:1152].bitcast(FP8X4), scales=p_scales[:, 1024:1152], in_=w_t[:, 4096:4608]
+                out=p_codes[:, 1024:1152].bitcast(FP8X4), scales=p_scales[:, 1024:1152], in_=pg[:, 4096:4608]
             )
 
         def first_matmul(n, kk):
@@ -245,6 +274,8 @@ def tile_convexrelucnn_kernel(tc, x, G, v, w, out):
         for n in range(len(chunks)):
             for kk in range(5):
                 first_matmul(n, kk)
+                if n == 0 and kk == 2:
+                    subtract_on_tensor(0)
             regroup(n, True)
             first_matmul(n, 5)
             if n > 0:
@@ -257,6 +288,8 @@ def tile_convexrelucnn_kernel(tc, x, G, v, w, out):
             if n == 1:
                 for par in range(2):
                     transpose_unit("G", 1, par)
+            if n + 1 < len(chunks):
+                subtract_on_tensor(n + 1)
             regroup(n, False)
             quantise_a(n, 0)
             quantise_p(n)

@@ -155,15 +155,17 @@ def tile_convexrelucnn_kernel(tc, x, G, v, w, out):
 
         def subtract_on_tensor(n):
             v_t, w_t = vw_tiles[n]
-            v_q = v_t[:].rearrange("p (t q) -> p q t", t=4)
-            w_q = w_t[:].rearrange("p (t q) -> p q t", t=4)
+            v_q = v_t[:].rearrange("p (t q) -> p t q", t=4)[:, :, ALU_COLS:]
+            w_q = w_t[:].rearrange("p (t q) -> p t q", t=4)[:, :, ALU_COLS:]
             pbank = psum.tile([P, 1024], BF16, name="pbank", tag="bank")
-            for h in range(PE_COLS // P):
-                cols = slice(ALU_COLS + h * P, ALU_COLS + (h + 1) * P)
-                dst = pbank[:, h * 512 : (h + 1) * 512].rearrange("p (q t) -> p q t", t=4)
-                nc.tensor.matmul(dst, lhsT=plus[:], rhs=v_q[:, cols], start=True, stop=False)
-                nc.tensor.matmul(dst, lhsT=minus[:], rhs=w_q[:, cols], start=False, stop=True)
-            nc.scalar.copy(out=p_grp(n)[:, 4 * ALU_COLS :], in_=pbank[:])
+            for h in range(2):
+                dst = pbank[:, h * 512 : (h + 1) * 512].rearrange("p (t q) -> p t q", t=2)
+                nc.tensor.matmul(dst, lhsT=plus[:], rhs=v_q[:, 2 * h : 2 * h + 2], start=True, stop=False)
+                nc.tensor.matmul(dst, lhsT=minus[:], rhs=w_q[:, 2 * h : 2 * h + 2], start=False, stop=True)
+            nc.scalar.copy(
+                out=p_grp(n)[:, 4 * ALU_COLS :].rearrange("p (q t) -> p q t", t=4),
+                in_=pbank[:].rearrange("p (t q) -> p q t", t=4),
+            )
 
         def p_grp(n):
             if n not in pg_of:

@@ -12,9 +12,8 @@ FP8X4 = mybir.dt.float8_e4m3fn_x4
 P = 128
 FLOPS = 2 * (128 * 27 * 1024 * 1024 + 128 * 27 * 1024 * 128)
 
-PE_COLS = 256
-ALU_COLS = 1152 - PE_COLS
-ACT_COLS = (128, 192)
+PE_COLS = (128, 128, 128, 128, 128, 128)
+ACT_COLS = (160, 160, 160, 224, 224, 224)
 VW_BUFS = 3
 J_ORDER = (0, 2, 1)
 
@@ -149,21 +148,27 @@ def tile_convexrelucnn_kernel(tc, x, G, v, w, out):
 
         def subtract(n):
             v_t, w_t = vw_tiles[n]
-            v_cols = v_t[:].rearrange("p (t q) -> p t q", t=4)[:, :, 0:ALU_COLS]
-            w_cols = w_t[:].rearrange("p (t q) -> p t q", t=4)[:, :, 0:ALU_COLS]
+            alu_cols = 1152 - PE_COLS[n]
+            v_cols = v_t[:].rearrange("p (t q) -> p t q", t=4)[:, :, 0:alu_cols]
+            w_cols = w_t[:].rearrange("p (t q) -> p t q", t=4)[:, :, 0:alu_cols]
             nc.vector.tensor_tensor(out=v_cols, in0=v_cols, in1=w_cols, op=mybir.AluOpType.subtract)
 
         def subtract_on_tensor(n):
+            if PE_COLS[n] == 0:
+                return
             v_t, w_t = vw_tiles[n]
-            v_q = v_t[:].rearrange("p (t q) -> p t q", t=4)[:, :, ALU_COLS:]
-            w_q = w_t[:].rearrange("p (t q) -> p t q", t=4)[:, :, ALU_COLS:]
-            pbank = psum.tile([P, 1024], BF16, name="pbank", tag="bank")
-            for h in range(2):
-                dst = pbank[:, h * 512 : (h + 1) * 512].rearrange("p (t q) -> p t q", t=2)
-                nc.tensor.matmul(dst, lhsT=plus[:], rhs=v_q[:, 2 * h : 2 * h + 2], start=True, stop=False)
-                nc.tensor.matmul(dst, lhsT=minus[:], rhs=w_q[:, 2 * h : 2 * h + 2], start=False, stop=True)
+            alu_cols = 1152 - PE_COLS[n]
+            v_q = v_t[:].rearrange("p (t q) -> p t q", t=4)[:, :, alu_cols:]
+            w_q = w_t[:].rearrange("p (t q) -> p t q", t=4)[:, :, alu_cols:]
+            pbank = psum.tile([P, 4 * PE_COLS[n]], BF16, name="pbank", tag="bank")
+            rows = 512 // PE_COLS[n]
+            for h in range(4 // rows):
+                dst = pbank[:, h * 512 : (h + 1) * 512].rearrange("p (t q) -> p t q", t=rows)
+                these = slice(rows * h, rows * (h + 1))
+                nc.tensor.matmul(dst, lhsT=plus[:], rhs=v_q[:, these], start=True, stop=False)
+                nc.tensor.matmul(dst, lhsT=minus[:], rhs=w_q[:, these], start=False, stop=True)
             nc.scalar.copy(
-                out=p_grp(n)[:, 4 * ALU_COLS :].rearrange("p (q t) -> p q t", t=4),
+                out=p_grp(n)[:, 4 * alu_cols :].rearrange("p (q t) -> p q t", t=4),
                 in_=pbank[:].rearrange("p (t q) -> p q t", t=4),
             )
 
@@ -175,8 +180,9 @@ def tile_convexrelucnn_kernel(tc, x, G, v, w, out):
 
         def regroup(n, on_scalar):
             v_t = vw_tiles[n][0]
-            split = ALU_COLS - ACT_COLS[chunks[n][0]]
-            lo, hi = (split, ALU_COLS) if on_scalar else (0, split)
+            alu_cols = 1152 - PE_COLS[n]
+            split = alu_cols - ACT_COLS[n]
+            lo, hi = (split, alu_cols) if on_scalar else (0, split)
             dst = p_grp(n)[:, 4 * lo : 4 * hi].rearrange("p (q i t) -> p q t i", i=4, t=4)
             src = v_t[:].rearrange("p (t q) -> p t q", t=4)[:, :, lo:hi].rearrange("p t (q i) -> p q t i", i=4)
             if on_scalar:

@@ -183,8 +183,8 @@ def tile_convexrelucnn_kernel(tc, x, G, v, w, out):
             alu_cols = 1152 - PE_COLS[n]
             split = alu_cols - ACT_COLS[n]
             lo, hi = (split, alu_cols) if on_scalar else (0, split)
-            dst = p_grp(n)[:, 4 * lo : 4 * hi].rearrange("p (q i t) -> p q t i", i=4, t=4)
-            src = v_t[:].rearrange("p (t q) -> p t q", t=4)[:, :, lo:hi].rearrange("p t (q i) -> p q t i", i=4)
+            dst = p_grp(n)[:, 4 * lo : 4 * hi].rearrange("p (q i t) -> p q t i", i=8, t=4)
+            src = v_t[:].rearrange("p (t q) -> p t q", t=4)[:, :, lo:hi].rearrange("p t (q i) -> p q t i", i=8)
             if on_scalar:
                 nc.scalar.copy(out=dst, in_=src)
             else:

from contextlib import ExitStack

import concourse.mybir as mybir
from concourse.masks import make_identity

F32 = mybir.dt.float32
BF16 = mybir.dt.bfloat16
U32 = mybir.dt.uint32
U8 = mybir.dt.uint8
FP8X4 = mybir.dt.float8_e4m3fn_x4

P = 128
FLOPS = 2 * (128 * 27 * 1024 * 1024 + 128 * 27 * 1024 * 128)

PE_COLS = (128, 128, 128, 128, 128, 128)
ACT_COLS = (160, 160, 160, 224, 224, 224)
VW_BUFS = 3
J_ORDER = (0, 2, 1)


def tile_convexrelucnn_kernel(tc, x, G, v, w, out):
    nc = tc.nc
    with ExitStack() as ctx:
        const = ctx.enter_context(tc.tile_pool(name="const", bufs=1))
        stage = ctx.enter_context(tc.tile_pool(name="stage", bufs=3))
        vw = ctx.enter_context(tc.tile_pool(name="vw", bufs=VW_BUFS))
        psum = ctx.enter_context(tc.psum_pool(name="psum", bufs=7))
        psum_acc = ctx.enter_context(tc.psum_pool(name="psum_acc", bufs=1))
        ctx.enter_context(tc.manual_schedule())

        chunks = [(g, c) for g in range(2) for c in range(3)]

        x_rows = x.rearrange("b c r s -> b c (r s)")
        g_rows = G.rearrange("(g p t) n -> p g (t n)", g=2, t=4)
        v_rows = v.rearrange("(g p t) k o -> p g t (k o)", g=2, t=4)
        w_rows = w.rearrange("(g p t) k o -> p g t (k o)", g=2, t=4)
        x_raw = {}
        g_raw = {}
        xj = {}
        gd = {}
        vw_tiles = {}
        grp_of = {}
        a_of = {}
        p_of = {}
        ag_of = {}
        pg_of = {}

        def load_x(c):
            xr = const.tile([P, 1156], BF16, name="x_raw%d" % c)
            nc.sync.dma_start(out=xr[:], in_=x_rows[:, c, :])
            x_raw[c] = xr

        def load_g(g):
            gr = const.tile([P, 4096], BF16, name="g_raw%d" % g)
            nc.sync.dma_start(out=gr[:], in_=g_rows[:, g, :])
            g_raw[g] = gr

        def load_chunk(n):
            g, c = chunks[n]
            v_t = vw.tile([P, 4608], BF16, name="v_t", tag="v_t", align_bytes=64)
            w_t = vw.tile([P, 4608], BF16, name="w_t", tag="w_t", align_bytes=64)
            nc.sync.dma_start(
                out=v_t[:].rearrange("p (t q) -> p t q", t=4),
                in_=v_rows[:, g, :, 1152 * c : 1152 * (c + 1)],
            )
            nc.sync.dma_start(
                out=w_t[:].rearrange("p (t q) -> p t q", t=4),
                in_=w_rows[:, g, :, 1152 * c : 1152 * (c + 1)],
            )
            vw_tiles[n] = (v_t, w_t)

        load_x(0)
        load_x(1)
        load_x(2)
        load_g(0)
        load_chunk(0)
        load_g(1)
        for n in range(1, VW_BUFS):
            load_chunk(n)

        ident = const.tile([P, P], F32, name="ident")
        make_identity(nc, ident[:])
        plus = const.tile([P, P], BF16, name="plus")
        minus = const.tile([P, P], BF16, name="minus")
        nc.gpsimd.tensor_copy(out=plus[:], in_=ident[:])
        nc.gpsimd.tensor_scalar(
            out=minus[:], in0=ident[:], scalar1=-1.0, scalar2=0.0, op0=mybir.AluOpType.mult, op1=mybir.AluOpType.add
        )

        g_codes = const.tile([P, 16 * P], U32, name="g_codes", align_bytes=64)
        g_scales = const.tile([P, 16 * P], U8, name="g_scales", align_bytes=64)
        u_codes = const.tile([P, 36 * P], U32, name="u_codes", align_bytes=64)
        u_scales = const.tile([P, 36 * P], U8, name="u_scales", align_bytes=64)
        acc = psum_acc.tile([P, P], F32, name="acc")

        def compact(c, j, on_scalar):
            if c not in xj:
                xj_c = const.tile([P, 3264], BF16, name="xj%d" % c, align_bytes=64)
                xj[c] = xj_c
            src = x_raw[c][:].rearrange("p (r2 par s) -> p par r2 s", par=2, s=34)
            dst = xj[c][:].rearrange("p (j par r2 wo) -> p j par r2 wo", j=3, par=2, wo=32)
            if on_scalar:
                nc.scalar.copy(out=dst[:, j], in_=src[:, :, :, j : j + 32])
            else:
                nc.vector.tensor_copy(out=dst[:, j], in_=src[:, :, :, j : j + 32])

        def split_g(g):
            gd_g = const.tile([P, 4096], BF16, name="g_split%d" % g, align_bytes=64)
            gd[g] = gd_g
            src = g_raw[g][:].rearrange("p (t a par wo) -> p t par a wo", t=4, par=2, wo=32)
            dst = gd_g[:].rearrange("p (t par a wo) -> p t par a wo", t=4, par=2, wo=32)
            for par in range(2):
                nc.vector.tensor_copy(out=dst[:, :, par], in_=src[:, :, par])

        def transpose_unit(kind, a, b):
            if kind == "U":
                words = xj[a][:].bitcast(F32)
                offsets = [((b * 2 + rho % 2) * 17 + rho // 2) * 16 for rho in range(4)]
            else:
                words = gd[a][:].bitcast(F32)
                offsets = [(t * 2 + b) * 256 for t in range(4)]
            grp = stage.tile([P, 2048], BF16, name="grp", tag="grp", bufs=4, align_bytes=64)
            grp_of[(kind, a, b)] = grp
            grp_w = grp[:].bitcast(F32).rearrange("p (s b u) -> p s b u", s=4, u=2)
            for h in range(2):
                bank = psum.tile([P, 512], F32, name="bank", tag="bank")
                for s in range(2):
                    for u in range(2):
                        off = offsets[2 * h + s] + P * u
                        col = (2 * s + u) * P
                        nc.tensor.transpose(bank[:, col : col + P], words[:, off : off + P], ident[:])
                nc.scalar.copy(
                    out=grp_w[:, 2 * h : 2 * h + 2],
                    in_=bank[:].rearrange("p (s u b) -> p s b u", s=2, u=2),
                )

        def quantise_unit(kind, a, b):
            grp = grp_of[(kind, a, b)]
            if kind == "U":
                lo = (a * 3 + b) * 512
                codes, scales = u_codes, u_scales
            else:
                lo = (b * 2 + a) * 512
                codes, scales = g_codes, g_scales
            nc.vector.quantize_mx(
                out=codes[:, lo : lo + 512].bitcast(FP8X4), scales=scales[:, lo : lo + 512], in_=grp[:]
            )

        def subtract(n):
            v_t, w_t = vw_tiles[n]
            alu_cols = 1152 - PE_COLS[n]
            v_cols = v_t[:].rearrange("p (t q) -> p t q", t=4)[:, :, 0:alu_cols]
            w_cols = w_t[:].rearrange("p (t q) -> p t q", t=4)[:, :, 0:alu_cols]
            nc.vector.tensor_tensor(out=v_cols, in0=v_cols, in1=w_cols, op=mybir.AluOpType.subtract)

        def subtract_on_tensor(n):
            if PE_COLS[n] == 0:
                return
            v_t, w_t = vw_tiles[n]
            alu_cols = 1152 - PE_COLS[n]
            v_q = v_t[:].rearrange("p (t q) -> p t q", t=4)[:, :, alu_cols:]
            w_q = w_t[:].rearrange("p (t q) -> p t q", t=4)[:, :, alu_cols:]
            pbank = psum.tile([P, 4 * PE_COLS[n]], BF16, name="pbank", tag="bank")
            rows = 512 // PE_COLS[n]
            for h in range(4 // rows):
                dst = pbank[:, h * 512 : (h + 1) * 512].rearrange("p (t q) -> p t q", t=rows)
                these = slice(rows * h, rows * (h + 1))
                nc.tensor.matmul(dst, lhsT=plus[:], rhs=v_q[:, these], start=True, stop=False)
                nc.tensor.matmul(dst, lhsT=minus[:], rhs=w_q[:, these], start=False, stop=True)
            nc.scalar.copy(
                out=p_grp(n)[:, 4 * alu_cols :].rearrange("p (q t) -> p q t", t=4),
                in_=pbank[:].rearrange("p (t q) -> p q t", t=4),
            )

        def p_grp(n):
            if n not in pg_of:
                pg = stage.tile([P, 4608], BF16, name="pg", tag="pg", bufs=2, align_bytes=64)
                pg_of[n] = pg
            return pg_of[n]

        def regroup(n, on_scalar):
            v_t = vw_tiles[n][0]
            alu_cols = 1152 - PE_COLS[n]
            split = alu_cols - ACT_COLS[n]
            lo, hi = (split, alu_cols) if on_scalar else (0, split)
            dst = p_grp(n)[:, 4 * lo : 4 * hi].rearrange("p (q i t) -> p q t i", i=8, t=4)
            src = v_t[:].rearrange("p (t q) -> p t q", t=4)[:, :, lo:hi].rearrange("p t (q i) -> p q t i", i=8)
            if on_scalar:
                nc.scalar.copy(out=dst, in_=src)
            else:
                nc.vector.tensor_copy(out=dst, in_=src)

        def quantise_p(n):
            pg = p_grp(n)
            p_codes = stage.tile([P, 1152], U32, name="p_codes", tag="p_codes", align_bytes=64)
            p_scales = stage.tile([P, 1152], U8, name="p_scales", tag="p_scales", align_bytes=64)
            p_of[n] = (p_codes, p_scales)
            nc.vector.quantize_mx(
                out=p_codes[:, 0:1024].bitcast(FP8X4), scales=p_scales[:, 0:1024], in_=pg[:, 0:4096]
            )
            nc.vector.quantize_mx(
                out=p_codes[:, 1024:1152].bitcast(FP8X4), scales=p_scales[:, 1024:1152], in_=pg[:, 4096:4608]
            )

        def first_matmul(n, kk):
            g, c = chunks[n]
            if kk % 4 == 0:
                ag = stage.tile([P, 2048], BF16, name="ag", tag="ag", bufs=4, align_bytes=64)
                ag_of[(n, kk // 4)] = ag
            ag = ag_of[(n, kk // 4)]
            s = kk % 4
            i, j = divmod(kk, 3)
            bank = psum.tile([P, 512], F32, name="bank", tag="bank")
            for t in range(4):
                for par in range(2):
                    gi = ((par * 2 + g) * 4 + t) * P
                    ui = ((c * 3 + j) * 4 + i + par) * P
                    nc.tensor.matmul_mx(
                        out=bank[:, t * P : (t + 1) * P],
                        lhsT=g_codes[:, gi : gi + P].bitcast(FP8X4),
                        lhsT_scale=g_scales[:, gi : gi + P],
                        rhs=u_codes[:, ui : ui + P].bitcast(FP8X4),
                        rhs_scale=u_scales[:, ui : ui + P],
                        start=(par == 0),
                        stop=(par == 1),
                    )
            nc.scalar.copy(
                out=ag[:, s * 512 : (s + 1) * 512].rearrange("p (b t) -> p b t", t=4),
                in_=bank[:].rearrange("p (t b) -> p b t", t=4),
            )

        def quantise_a(n, grp_i):
            if grp_i == 0:
                a_codes = stage.tile([P, 1152], U32, name="a_codes", tag="a_codes", align_bytes=64)
                a_scales = stage.tile([P, 1152], U8, name="a_scales", tag="a_scales", align_bytes=64)
                a_of[n] = (a_codes, a_scales)
            a_codes, a_scales = a_of[n]
            count = 4 if grp_i < 2 else 1
            lo = grp_i * 512
            nc.vector.quantize_mx(
                out=a_codes[:, lo : lo + count * P].bitcast(FP8X4),
                scales=a_scales[:, lo : lo + count * P],
                in_=ag_of[(n, grp_i)][:, 0 : count * 512],
            )

        def second_matmul(n):
            a_codes, a_scales = a_of[n]
            p_codes, p_scales = p_of[n]
            for kk in range(9):
                cols = slice(kk * P, (kk + 1) * P)
                nc.tensor.matmul_mx(
                    out=acc[:],
                    lhsT=a_codes[:, cols].bitcast(FP8X4),
                    lhsT_scale=a_scales[:, cols],
                    rhs=p_codes[:, cols].bitcast(FP8X4),
                    rhs_scale=p_scales[:, cols],
                    start=(n == 0 and kk == 0),
                    stop=(n == len(chunks) - 1 and kk == 8),
                )

        compact(0, 0, False)
        compact(0, 2, False)
        compact(0, 1, True)
        for j in J_ORDER:
            transpose_unit("U", 0, j)
        for c in (1, 2):
            for j in J_ORDER:
                compact(c, j, False)
        split_g(0)
        for j in J_ORDER:
            quantise_unit("U", 0, j)
        for par in range(2):
            transpose_unit("G", 0, par)
        for par in range(2):
            quantise_unit("G", 0, par)
        for j in J_ORDER:
            transpose_unit("U", 1, j)
        subtract(0)
        for j in J_ORDER:
            quantise_unit("U", 1, j)

        for n in range(len(chunks)):
            for kk in range(5):
                first_matmul(n, kk)
                if n == 0 and kk == 2:
                    subtract_on_tensor(0)
            regroup(n, True)
            first_matmul(n, 5)
            if n > 0:
                second_matmul(n - 1)
            for kk in range(6, 9):
                first_matmul(n, kk)
            if n == 0:
                for j in J_ORDER:
                    transpose_unit("U", 2, j)
            if n == 1:
                for par in range(2):
                    transpose_unit("G", 1, par)
            if n + 1 < len(chunks):
                subtract_on_tensor(n + 1)
            regroup(n, False)
            quantise_a(n, 0)
            quantise_p(n)
            if n + VW_BUFS < len(chunks):
                load_chunk(n + VW_BUFS)
            if n == 0:
                split_g(1)
            if n + 1 < len(chunks):
                subtract(n + 1)
            if n == 0:
                for j in J_ORDER:
                    quantise_unit("U", 2, j)
            if n == 1:
                for par in range(2):
                    quantise_unit("G", 1, par)
            quantise_a(n, 1)
            quantise_a(n, 2)
        second_matmul(len(chunks) - 1)

        res = const.tile([P, P], F32, name="res")
        nc.vector.tensor_copy(out=res[:], in_=acc[:])
        nc.sync.dma_start(out=out[:, :], in_=res[:])
